import numpy as np
import ml_dtypes

BF16 = ml_dtypes.bfloat16


def bf(x):
    return np.asarray(x, np.float32).astype(BF16)


def f32(x):
    return np.asarray(x, np.float32)


def f64(x):
    return np.asarray(x).astype(np.float64)


def striped(idx):
    return np.tile(idx.reshape(-1, 16).T, (8, 1))


D, S, M, N = 128, 256, 512, 64
LN_EPS = 1e-5


def setup_inputs():
    return {"table": bf(0.5 + 2.0 * np.random.standard_normal((D, S))), "w": bf(np.random.standard_normal((D, M)) / np.sqrt(D)), "offs": striped(np.random.permutation(np.tile(np.arange(S), 2))[:N])}


def reference(table, w, offs):
    idx = offs[:16].T.reshape(-1)
    t = f64(table)
    mu = t.mean(axis=0, keepdims=True)
    var = ((t - mu) ** 2).mean(axis=0, keepdims=True)
    xn = (t - mu) / np.sqrt(var + LN_EPS)
    return np.maximum(f64(w).T @ xn[:, idx], 0.0)

@@ -1,0 +1,68 @@
+import concourse.mybir as mybir
+
+BF16, F32, U16 = mybir.dt.bfloat16, mybir.dt.float32, mybir.dt.uint16
+ACT = mybir.ActivationFunctionType
+ALU = mybir.AluOpType
+
+P = 128
+WORDS = 256
+NEURONS = 512
+HEADS = NEURONS // P
+TOKENS = 64
+LN_EPS = 1e-5
+
+FLOPS = 2 * P * NEURONS * TOKENS
+
+
+def tile_bdhencoder_kernel(tc, table, w, offs, out):
+    nc = tc.nc
+    with tc.tile_pool(name="held", bufs=1) as held, tc.psum_pool(name="psum", bufs=1) as psum:
+        raw = held.tile([P, WORDS], BF16, name="raw")
+        offsets = held.tile([P, TOKENS // 16], U16, name="offsets")
+        weights = held.tile([P, NEURONS], BF16, name="weights")
+        nc.sync.dma_start(raw[:], table)
+        nc.sync.dma_start(offsets[:], offs)
+        nc.scalar.dma_start(weights[:], w)
+
+        centring = held.tile([P, P], BF16, name="centring")
+        nc.gpsimd.memset(centring[:], -1.0 / P)
+        nc.gpsimd.affine_select(
+            out=centring[:],
+            in_=centring[:],
+            compare_op=ALU.not_equal,
+            fill=1.0 - 1.0 / P,
+            base=0,
+            pattern=[[-1, P]],
+            channel_multiplier=1,
+        )
+        averaging = held.tile([P, P], F32, name="averaging")
+        nc.vector.memset(averaging[:], 1.0 / P)
+        eps = held.tile([P, 1], F32, name="eps")
+        nc.vector.memset(eps[:], LN_EPS)
+
+        centred = psum.tile([P, WORDS], F32, name="centred")
+        nc.tensor.matmul(centred[:], centring[:], raw[:], start=True, stop=True)
+        squares = held.tile([P, WORDS], F32, name="squares")
+        nc.scalar.activation(squares[:], centred[:], ACT.Square)
+        variance = psum.tile([P, WORDS], F32, name="variance")
+        nc.tensor.matmul(variance[:], averaging[:], squares[:], start=True, stop=True)
+
+        deviation = held.tile([P, WORDS], F32, name="deviation")
+        nc.scalar.activation(deviation[:], variance[:], ACT.Sqrt, bias=eps[:])
+        inverse = held.tile([P, WORDS], F32, name="inverse")
+        nc.vector.reciprocal(inverse[:], deviation[:])
+        normalised = held.tile([P, WORDS], BF16, name="normalised")
+        nc.vector.tensor_tensor(normalised[:], centred[:], inverse[:], ALU.mult)
+
+        projected = psum.tile([P, HEADS, TOKENS], F32, name="projected")
+        for h in range(HEADS):
+            nc.tensor.matmul(
+                projected[:, h, :],
+                weights[:, h * P : (h + 1) * P],
+                normalised[:].indirect(offsets[:]),
+                start=True,
+                stop=True,
+            )
+        result = held.tile([P, HEADS, TOKENS], F32, name="result")
+        nc.vector.tensor_scalar_max(result[:], projected[:], 0.0)
+        nc.sync.dma_start(out.rearrange("(h p) j -> p h j", p=P), result[:])

@@ -47,10 +47,8 @@ def tile_bdhencoder_kernel(tc, table, w, offs, out):
         variance = psum.tile([P, WORDS], F32, name="variance")
         nc.tensor.matmul(variance[:], averaging[:], squares[:], start=True, stop=True)
 
-        deviation = held.tile([P, WORDS], F32, name="deviation")
-        nc.scalar.activation(deviation[:], variance[:], ACT.Sqrt, bias=eps[:])
         inverse = held.tile([P, WORDS], F32, name="inverse")
-        nc.vector.reciprocal(inverse[:], deviation[:])
+        nc.scalar.activation(inverse[:], variance[:], ACT.Abs_reciprocal_sqrt, bias=eps[:])
         normalised = held.tile([P, WORDS], BF16, name="normalised")
         nc.vector.tensor_tensor(normalised[:], centred[:], inverse[:], ALU.mult)
 

@@ -39,6 +39,8 @@ def tile_bdhencoder_kernel(tc, table, w, offs, out):
         nc.vector.memset(averaging[:], 1.0 / P)
         eps = held.tile([P, 1], F32, name="eps")
         nc.vector.memset(eps[:], LN_EPS)
+        primed = held.tile([P, 1], F32, name="primed")
+        nc.scalar.activation(primed[:], eps[:], ACT.Abs_reciprocal_sqrt)
 
         centred = psum.tile([P, WORDS], F32, name="centred")
         nc.tensor.matmul(centred[:], centring[:], raw[:], start=True, stop=True)

@@ -8,6 +8,7 @@ P = 128
 WORDS = 256
 NEURONS = 512
 HEADS = NEURONS // P
+HALF = WORDS // 2
 TOKENS = 64
 LN_EPS = 1e-5
 
@@ -42,27 +43,37 @@ def tile_bdhencoder_kernel(tc, table, w, offs, out):
         primed = held.tile([P, 1], F32, name="primed")
         nc.scalar.activation(primed[:], eps[:], ACT.Abs_reciprocal_sqrt)
 
-        centred = psum.tile([P, WORDS], F32, name="centred")
-        nc.tensor.matmul(centred[:], centring[:], raw[:], start=True, stop=True)
+        halves = [slice(c * HALF, (c + 1) * HALF) for c in range(2)]
+        centred = [psum.tile([P, HALF], F32, name=f"centred{c}") for c in range(2)]
+        variance = [psum.tile([P, HALF], F32, name=f"variance{c}") for c in range(2)]
         squares = held.tile([P, WORDS], F32, name="squares")
-        nc.scalar.activation(squares[:], centred[:], ACT.Square)
-        variance = psum.tile([P, WORDS], F32, name="variance")
-        nc.tensor.matmul(variance[:], averaging[:], squares[:], start=True, stop=True)
-
         inverse = held.tile([P, WORDS], F32, name="inverse")
-        nc.scalar.activation(inverse[:], variance[:], ACT.Abs_reciprocal_sqrt, bias=eps[:])
         normalised = held.tile([P, WORDS], BF16, name="normalised")
-        nc.vector.tensor_tensor(normalised[:], centred[:], inverse[:], ALU.mult)
+        for c, half in enumerate(halves):
+            nc.tensor.matmul(centred[c][:], centring[:], raw[:, half], start=True, stop=True)
+        for c, half in enumerate(halves):
+            nc.scalar.activation(squares[:, half], centred[c][:], ACT.Square)
+        for c, half in enumerate(halves):
+            nc.tensor.matmul(variance[c][:], averaging[:], squares[:, half], start=True, stop=True)
+        for c, half in enumerate(halves):
+            nc.scalar.activation(inverse[:, half], variance[c][:], ACT.Abs_reciprocal_sqrt, bias=eps[:])
+        for c, half in enumerate(halves):
+            nc.vector.tensor_tensor(normalised[:, half], centred[c][:], inverse[:, half], ALU.mult)
 
-        projected = psum.tile([P, HEADS, TOKENS], F32, name="projected")
+        by_head = out.rearrange("(h p) j -> h p j", p=P)
         for h in range(HEADS):
+            projected = psum.tile([P, TOKENS], F32, name=f"projected{h}")
             nc.tensor.matmul(
-                projected[:, h, :],
+                projected[:],
                 weights[:, h * P : (h + 1) * P],
                 normalised[:].indirect(offsets[:]),
                 start=True,
                 stop=True,
             )
-        result = held.tile([P, HEADS, TOKENS], F32, name="result")
-        nc.vector.tensor_scalar_max(result[:], projected[:], 0.0)
-        nc.sync.dma_start(out.rearrange("(h p) j -> p h j", p=P), result[:])
+            result = held.tile([P, TOKENS], F32, name=f"result{h}")
+            if h % 2 == 0:
+                nc.vector.tensor_scalar_max(result[:], projected[:], 0.0)
+                nc.sync.dma_start(by_head[h], result[:])
+            else:
+                nc.scalar.activation(result[:], projected[:], ACT.Relu)
+                nc.scalar.dma_start(by_head[h], result[:])

@@ -8,7 +8,6 @@ P = 128
 WORDS = 256
 NEURONS = 512
 HEADS = NEURONS // P
-HALF = WORDS // 2
 TOKENS = 64
 LN_EPS = 1e-5
 
@@ -43,22 +42,17 @@ def tile_bdhencoder_kernel(tc, table, w, offs, out):
         primed = held.tile([P, 1], F32, name="primed")
         nc.scalar.activation(primed[:], eps[:], ACT.Abs_reciprocal_sqrt)
 
-        halves = [slice(c * HALF, (c + 1) * HALF) for c in range(2)]
-        centred = [psum.tile([P, HALF], F32, name=f"centred{c}") for c in range(2)]
-        variance = [psum.tile([P, HALF], F32, name=f"variance{c}") for c in range(2)]
+        centred = psum.tile([P, WORDS], F32, name="centred")
+        nc.tensor.matmul(centred[:], centring[:], raw[:], start=True, stop=True)
         squares = held.tile([P, WORDS], F32, name="squares")
+        nc.scalar.activation(squares[:], centred[:], ACT.Square)
+        variance = psum.tile([P, WORDS], F32, name="variance")
+        nc.tensor.matmul(variance[:], averaging[:], squares[:], start=True, stop=True)
+
         inverse = held.tile([P, WORDS], F32, name="inverse")
+        nc.scalar.activation(inverse[:], variance[:], ACT.Abs_reciprocal_sqrt, bias=eps[:])
         normalised = held.tile([P, WORDS], BF16, name="normalised")
-        for c, half in enumerate(halves):
-            nc.tensor.matmul(centred[c][:], centring[:], raw[:, half], start=True, stop=True)
-        for c, half in enumerate(halves):
-            nc.scalar.activation(squares[:, half], centred[c][:], ACT.Square)
-        for c, half in enumerate(halves):
-            nc.tensor.matmul(variance[c][:], averaging[:], squares[:, half], start=True, stop=True)
-        for c, half in enumerate(halves):
-            nc.scalar.activation(inverse[:, half], variance[c][:], ACT.Abs_reciprocal_sqrt, bias=eps[:])
-        for c, half in enumerate(halves):
-            nc.vector.tensor_tensor(normalised[:, half], centred[c][:], inverse[:, half], ALU.mult)
+        nc.vector.tensor_tensor(normalised[:], centred[:], inverse[:], ALU.mult)
 
         by_head = out.rearrange("(h p) j -> h p j", p=P)
         for h in range(HEADS):

@@ -1,3 +1,5 @@
+from contextlib import ExitStack
+
 import concourse.mybir as mybir
 
 BF16, F32, U16 = mybir.dt.bfloat16, mybir.dt.float32, mybir.dt.uint16
@@ -8,21 +10,31 @@ P = 128
 WORDS = 256
 NEURONS = 512
 HEADS = NEURONS // P
+HALF = WORDS // 2
 TOKENS = 64
 LN_EPS = 1e-5
+WARMUPS = 6
 
 FLOPS = 2 * P * NEURONS * TOKENS
 
 
 def tile_bdhencoder_kernel(tc, table, w, offs, out):
     nc = tc.nc
-    with tc.tile_pool(name="held", bufs=1) as held, tc.psum_pool(name="psum", bufs=1) as psum:
+    with ExitStack() as ctx:
+        held = ctx.enter_context(tc.tile_pool(name="held", bufs=1))
         raw = held.tile([P, WORDS], BF16, name="raw")
         offsets = held.tile([P, TOKENS // 16], U16, name="offsets")
         weights = held.tile([P, NEURONS], BF16, name="weights")
         nc.sync.dma_start(raw[:], table)
         nc.sync.dma_start(offsets[:], offs)
         nc.scalar.dma_start(weights[:], w)
+
+        zeros = held.tile([P, WORDS], BF16, name="zeros")
+        nc.vector.memset(zeros[:], 0.0)
+        with tc.psum_pool(name="idle", bufs=1) as idle:
+            unread = idle.tile([P, WORDS], F32, name="unread")
+            for i in range(WARMUPS):
+                nc.tensor.matmul(unread[:], zeros[:, :P], zeros[:], start=True, stop=True)
 
         centring = held.tile([P, P], BF16, name="centring")
         nc.gpsimd.memset(centring[:], -1.0 / P)
@@ -42,17 +54,23 @@ def tile_bdhencoder_kernel(tc, table, w, offs, out):
         primed = held.tile([P, 1], F32, name="primed")
         nc.scalar.activation(primed[:], eps[:], ACT.Abs_reciprocal_sqrt)
 
-        centred = psum.tile([P, WORDS], F32, name="centred")
-        nc.tensor.matmul(centred[:], centring[:], raw[:], start=True, stop=True)
+        psum = ctx.enter_context(tc.psum_pool(name="psum", bufs=1))
+        halves = [slice(c * HALF, (c + 1) * HALF) for c in range(2)]
+        centred = [psum.tile([P, HALF], F32, name=f"centred{c}") for c in range(2)]
+        variance = [psum.tile([P, HALF], F32, name=f"variance{c}") for c in range(2)]
         squares = held.tile([P, WORDS], F32, name="squares")
-        nc.scalar.activation(squares[:], centred[:], ACT.Square)
-        variance = psum.tile([P, WORDS], F32, name="variance")
-        nc.tensor.matmul(variance[:], averaging[:], squares[:], start=True, stop=True)
-
         inverse = held.tile([P, WORDS], F32, name="inverse")
-        nc.scalar.activation(inverse[:], variance[:], ACT.Abs_reciprocal_sqrt, bias=eps[:])
         normalised = held.tile([P, WORDS], BF16, name="normalised")
-        nc.vector.tensor_tensor(normalised[:], centred[:], inverse[:], ALU.mult)
+        for c, half in enumerate(halves):
+            nc.tensor.matmul(centred[c][:], centring[:], raw[:, half], start=True, stop=True)
+        for c, half in enumerate(halves):
+            nc.scalar.activation(squares[:, half], centred[c][:], ACT.Square)
+        for c, half in enumerate(halves):
+            nc.tensor.matmul(variance[c][:], averaging[:], squares[:, half], start=True, stop=True)
+        for c, half in enumerate(halves):
+            nc.scalar.activation(inverse[:, half], variance[c][:], ACT.Abs_reciprocal_sqrt, bias=eps[:])
+        for c, half in enumerate(halves):
+            nc.vector.tensor_tensor(normalised[:, half], centred[c][:], inverse[:, half], ALU.mult)
 
         by_head = out.rearrange("(h p) j -> h p j", p=P)
         for h in range(HEADS):

@@ -13,7 +13,7 @@ HEADS = NEURONS // P
 HALF = WORDS // 2
 TOKENS = 64
 LN_EPS = 1e-5
-WARMUPS = 6
+WARMUPS = 4
 
 FLOPS = 2 * P * NEURONS * TOKENS
 

@@ -25,7 +25,8 @@ def tile_bdhencoder_kernel(tc, table, w, offs, out):
         raw = held.tile([P, WORDS], BF16, name="raw")
         offsets = held.tile([P, TOKENS // 16], U16, name="offsets")
         weights = held.tile([P, NEURONS], BF16, name="weights")
-        nc.sync.dma_start(raw[:], table)
+        nc.sync.dma_start(raw[: P // 2, :], table[: P // 2, :])
+        nc.scalar.dma_start(raw[P // 2 :, :], table[P // 2 :, :])
         nc.sync.dma_start(offsets[:], offs)
         nc.scalar.dma_start(weights[:], w)
 

@@ -13,7 +13,8 @@ HEADS = NEURONS // P
 HALF = WORDS // 2
 TOKENS = 64
 LN_EPS = 1e-5
-WARMUPS = 4
+WARMUPS = 2
+WARMUP_COLUMNS = 512
 
 FLOPS = 2 * P * NEURONS * TOKENS
 
@@ -30,10 +31,10 @@ def tile_bdhencoder_kernel(tc, table, w, offs, out):
         nc.sync.dma_start(offsets[:], offs)
         nc.scalar.dma_start(weights[:], w)
 
-        zeros = held.tile([P, WORDS], BF16, name="zeros")
+        zeros = held.tile([P, WARMUP_COLUMNS], BF16, name="zeros")
         nc.vector.memset(zeros[:], 0.0)
         with tc.psum_pool(name="idle", bufs=1) as idle:
-            unread = idle.tile([P, WORDS], F32, name="unread")
+            unread = idle.tile([P, WARMUP_COLUMNS], F32, name="unread")
             for i in range(WARMUPS):
                 nc.tensor.matmul(unread[:], zeros[:, :P], zeros[:], start=True, stop=True)
 
@@ -65,7 +66,7 @@ def tile_bdhencoder_kernel(tc, table, w, offs, out):
         for c, half in enumerate(halves):
             nc.tensor.matmul(centred[c][:], centring[:], raw[:, half], start=True, stop=True)
         for c, half in enumerate(halves):
-            nc.scalar.activation(squares[:, half], centred[c][:], ACT.Square)
+            nc.vector.tensor_tensor(squares[:, half], centred[c][:], raw[:, half], ALU.mult)
         for c, half in enumerate(halves):
             nc.tensor.matmul(variance[c][:], averaging[:], squares[:, half], start=True, stop=True)
         for c, half in enumerate(halves):

@@ -85,9 +85,6 @@ def tile_bdhencoder_kernel(tc, table, w, offs, out):
                 stop=True,
             )
             result = held.tile([P, TOKENS], F32, name=f"result{h}")
-            if h % 2 == 0:
-                nc.vector.tensor_scalar_max(result[:], projected[:], 0.0)
-                nc.sync.dma_start(by_head[h], result[:])
-            else:
-                nc.scalar.activation(result[:], projected[:], ACT.Relu)
-                nc.scalar.dma_start(by_head[h], result[:])
+            nc.vector.tensor_scalar_max(result[:], projected[:], 0.0)
+            queue = nc.sync if h % 2 == 0 else nc.scalar
+            queue.dma_start(by_head[h], result[:])

@@ -14,7 +14,7 @@ HALF = WORDS // 2
 TOKENS = 64
 LN_EPS = 1e-5
 WARMUPS = 2
-WARMUP_COLUMNS = 512
+BLOCKS = 4
 
 FLOPS = 2 * P * NEURONS * TOKENS
 
@@ -31,12 +31,13 @@ def tile_bdhencoder_kernel(tc, table, w, offs, out):
         nc.sync.dma_start(offsets[:], offs)
         nc.scalar.dma_start(weights[:], w)
 
-        zeros = held.tile([P, WARMUP_COLUMNS], BF16, name="zeros")
+        zeros = held.tile([P, P], BF16, name="zeros")
         nc.vector.memset(zeros[:], 0.0)
         with tc.psum_pool(name="idle", bufs=1) as idle:
-            unread = idle.tile([P, WARMUP_COLUMNS], F32, name="unread")
+            unread = idle.tile([P, BLOCKS, P], F32, name="unread")
+            blocks = zeros[:].unsqueeze(1).to_broadcast([P, BLOCKS, P])
             for i in range(WARMUPS):
-                nc.tensor.matmul(unread[:], zeros[:, :P], zeros[:], start=True, stop=True)
+                nc.tensor.matmul(unread[:], zeros[:], blocks, start=True, stop=True)
 
         centring = held.tile([P, P], BF16, name="centring")
         nc.gpsimd.memset(centring[:], -1.0 / P)

@@ -87,5 +87,5 @@ def tile_bdhencoder_kernel(tc, table, w, offs, out):
             )
             result = held.tile([P, TOKENS], F32, name=f"result{h}")
             nc.vector.tensor_scalar_max(result[:], projected[:], 0.0)
-            queue = nc.sync if h % 2 == 0 else nc.scalar
+            queue = nc.scalar if h % 2 == 0 else nc.sync
             queue.dma_start(by_head[h], result[:])

@@ -10,7 +10,7 @@ P = 128
 WORDS = 256
 NEURONS = 512
 HEADS = NEURONS // P
-HALF = WORDS // 2
+QUARTER = WORDS // 4
 TOKENS = 64
 LN_EPS = 1e-5
 WARMUPS = 2
@@ -58,26 +58,29 @@ def tile_bdhencoder_kernel(tc, table, w, offs, out):
         nc.scalar.activation(primed[:], eps[:], ACT.Abs_reciprocal_sqrt)
 
         psum = ctx.enter_context(tc.psum_pool(name="psum", bufs=1))
-        halves = [slice(c * HALF, (c + 1) * HALF) for c in range(2)]
-        centred = [psum.tile([P, HALF], F32, name=f"centred{c}") for c in range(2)]
-        variance = [psum.tile([P, HALF], F32, name=f"variance{c}") for c in range(2)]
+        centred = [psum.tile([P, QUARTER], F32, name=f"centred{q}") for q in range(4)]
+        variance = [psum.tile([P, 2, QUARTER], F32, name=f"variance{c}") for c in range(2)]
         squares = held.tile([P, WORDS], F32, name="squares")
         inverse = held.tile([P, WORDS], F32, name="inverse")
         normalised = held.tile([P, WORDS], BF16, name="normalised")
-        for c, half in enumerate(halves):
-            nc.tensor.matmul(centred[c][:], centring[:], raw[:, half], start=True, stop=True)
-        for c, half in enumerate(halves):
-            nc.vector.tensor_tensor(squares[:, half], centred[c][:], raw[:, half], ALU.mult)
-        for c, half in enumerate(halves):
+        quarters = [slice(q * QUARTER, (q + 1) * QUARTER) for q in range(4)]
+        for q, words in enumerate(quarters):
+            nc.tensor.matmul(centred[q][:], centring[:], raw[:, words], start=True, stop=True)
+        for q, words in enumerate(quarters):
+            nc.vector.tensor_tensor(squares[:, words], centred[q][:], raw[:, words], ALU.mult)
+        for c in range(2):
+            half = slice(2 * c * QUARTER, 2 * (c + 1) * QUARTER)
             nc.tensor.matmul(variance[c][:], averaging[:], squares[:, half], start=True, stop=True)
-        for c, half in enumerate(halves):
-            nc.scalar.activation(inverse[:, half], variance[c][:], ACT.Abs_reciprocal_sqrt, bias=eps[:])
-        for c, half in enumerate(halves):
-            nc.vector.tensor_tensor(normalised[:, half], centred[c][:], inverse[:, half], ALU.mult)
+        for q, words in enumerate(quarters):
+            var = variance[q // 2][:, q % 2, :]
+            nc.scalar.activation(inverse[:, words], var, ACT.Abs_reciprocal_sqrt, bias=eps[:])
+        for q, words in enumerate(quarters):
+            nc.vector.tensor_tensor(normalised[:, words], centred[q][:], inverse[:, words], ALU.mult)
 
         by_head = out.rearrange("(h p) j -> h p j", p=P)
         for h in range(HEADS):
-            projected = psum.tile([P, TOKENS], F32, name=f"projected{h}")
+            tag = f"variance{h}" if h < 2 else f"projected{h}"
+            projected = psum.tile([P, TOKENS], F32, name=f"projected{h}", tag=tag)
             nc.tensor.matmul(
                 projected[:],
                 weights[:, h * P : (h + 1) * P],

from contextlib import ExitStack

import concourse.mybir as mybir

BF16, F32, U16 = mybir.dt.bfloat16, mybir.dt.float32, mybir.dt.uint16
ACT = mybir.ActivationFunctionType
ALU = mybir.AluOpType

P = 128
WORDS = 256
NEURONS = 512
HEADS = NEURONS // P
QUARTER = WORDS // 4
TOKENS = 64
LN_EPS = 1e-5
WARMUPS = 2
BLOCKS = 4

FLOPS = 2 * P * NEURONS * TOKENS


def tile_bdhencoder_kernel(tc, table, w, offs, out):
    nc = tc.nc
    with ExitStack() as ctx:
        held = ctx.enter_context(tc.tile_pool(name="held", bufs=1))
        raw = held.tile([P, WORDS], BF16, name="raw")
        offsets = held.tile([P, TOKENS // 16], U16, name="offsets")
        weights = held.tile([P, NEURONS], BF16, name="weights")
        nc.sync.dma_start(raw[: P // 2, :], table[: P // 2, :])
        nc.scalar.dma_start(raw[P // 2 :, :], table[P // 2 :, :])
        nc.sync.dma_start(offsets[:], offs)
        nc.scalar.dma_start(weights[:], w)

        zeros = held.tile([P, P], BF16, name="zeros")
        nc.vector.memset(zeros[:], 0.0)
        with tc.psum_pool(name="idle", bufs=1) as idle:
            unread = idle.tile([P, BLOCKS, P], F32, name="unread")
            blocks = zeros[:].unsqueeze(1).to_broadcast([P, BLOCKS, P])
            for i in range(WARMUPS):
                nc.tensor.matmul(unread[:], zeros[:], blocks, start=True, stop=True)

        centring = held.tile([P, P], BF16, name="centring")
        nc.gpsimd.memset(centring[:], -1.0 / P)
        nc.gpsimd.affine_select(
            out=centring[:],
            in_=centring[:],
            compare_op=ALU.not_equal,
            fill=1.0 - 1.0 / P,
            base=0,
            pattern=[[-1, P]],
            channel_multiplier=1,
        )
        averaging = held.tile([P, P], F32, name="averaging")
        nc.vector.memset(averaging[:], 1.0 / P)
        eps = held.tile([P, 1], F32, name="eps")
        nc.vector.memset(eps[:], LN_EPS)
        primed = held.tile([P, 1], F32, name="primed")
        nc.scalar.activation(primed[:], eps[:], ACT.Abs_reciprocal_sqrt)

        psum = ctx.enter_context(tc.psum_pool(name="psum", bufs=1))
        centred = [psum.tile([P, QUARTER], F32, name=f"centred{q}") for q in range(4)]
        variance = [psum.tile([P, 2, QUARTER], F32, name=f"variance{c}") for c in range(2)]
        squares = held.tile([P, WORDS], F32, name="squares")
        inverse = held.tile([P, WORDS], F32, name="inverse")
        normalised = held.tile([P, WORDS], BF16, name="normalised")
        quarters = [slice(q * QUARTER, (q + 1) * QUARTER) for q in range(4)]
        for q, words in enumerate(quarters):
            nc.tensor.matmul(centred[q][:], centring[:], raw[:, words], start=True, stop=True)
        for q, words in enumerate(quarters):
            nc.vector.tensor_tensor(squares[:, words], centred[q][:], raw[:, words], ALU.mult)
        for c in range(2):
            half = slice(2 * c * QUARTER, 2 * (c + 1) * QUARTER)
            nc.tensor.matmul(variance[c][:], averaging[:], squares[:, half], start=True, stop=True)
        for q, words in enumerate(quarters):
            var = variance[q // 2][:, q % 2, :]
            nc.scalar.activation(inverse[:, words], var, ACT.Abs_reciprocal_sqrt, bias=eps[:])
        for q, words in enumerate(quarters):
            nc.vector.tensor_tensor(normalised[:, words], centred[q][:], inverse[:, words], ALU.mult)

        by_head = out.rearrange("(h p) j -> h p j", p=P)
        for h in range(HEADS):
            tag = f"variance{h}" if h < 2 else f"projected{h}"
            projected = psum.tile([P, TOKENS], F32, name=f"projected{h}", tag=tag)
            nc.tensor.matmul(
                projected[:],
                weights[:, h * P : (h + 1) * P],
                normalised[:].indirect(offsets[:]),
                start=True,
                stop=True,
            )
            result = held.tile([P, TOKENS], F32, name=f"result{h}")
            nc.vector.tensor_scalar_max(result[:], projected[:], 0.0)
            queue = nc.scalar if h % 2 == 0 else nc.sync
            queue.dma_start(by_head[h], result[:])
